import numpy as np
import ml_dtypes


def mxq(x, axis, fmt="e4m3"):
    dtype, down = {"e4m3": (ml_dtypes.float8_e4m3fn, 7), "e5m2": (ml_dtypes.float8_e5m2, 14)}[fmt]
    v = np.moveaxis(np.asarray(x, np.float32).astype(ml_dtypes.bfloat16).astype(np.float64), axis, -1)
    blocks = v.reshape(v.shape[:-1] + (-1, 32))
    amax = np.abs(blocks).max(-1, keepdims=True)
    byte = np.maximum(np.where(amax > 0, np.frexp(amax)[1] - 1 + 127, 0) - down, 1)
    scale = np.exp2(byte - 127.0)
    codes = (blocks / scale).astype(np.float32).astype(dtype).astype(np.float64)
    return np.moveaxis((codes * scale).reshape(v.shape), -1, axis)


WIDE = False


def mx_kscale(k):
    if not WIDE:
        return np.ones(k)
    levels = np.array([10, -10, 5, -5, 0])
    a = np.random.permutation(np.resize(levels, k // 512 * 4)).reshape(k // 512, 4)
    idx = np.arange(k)
    return np.exp2(a[idx // 512, idx % 128 // 32])


BF16 = ml_dtypes.bfloat16


def bf(x):
    return np.asarray(x, np.float32).astype(BF16)


def f64(x):
    return np.asarray(x).astype(np.float64)


B, T, D, C, M = 4, 2048, 1024, 128, 4
NB = T // M
NEG = -1e30


def setup_inputs():
    s = mx_kscale(D)
    w = 1.0 / np.sqrt(D)
    return {
        "H": bf(np.random.standard_normal((B, T, D)) * s),
        "W_a_KV": bf(np.random.standard_normal((D, C)) * w / s[:, None]),
        "W_b_KV": bf(np.random.standard_normal((D, C)) * w / s[:, None]),
        "W_a_Z": bf(np.random.standard_normal((D, C)) * w / s[:, None]),
        "W_b_Z": bf(np.random.standard_normal((D, C)) * w / s[:, None]),
        "B_a": bf(np.random.standard_normal((M, C))),
        "B_b": bf(np.random.standard_normal((M, C))),
    }


def reference(H, W_a_KV, W_b_KV, W_a_Z, W_b_Z, B_a, B_b):
    Hq = mxq(f64(H), 2, "e4m3")
    C_a = (Hq @ mxq(f64(W_a_KV), 0, "e4m3")).reshape(B, NB, M, C)
    C_b = (Hq @ mxq(f64(W_b_KV), 0, "e4m3")).reshape(B, NB, M, C)
    Z_a = (Hq @ mxq(f64(W_a_Z), 0, "e4m3")).reshape(B, NB, M, C) + f64(B_a)
    Z_b = (Hq @ mxq(f64(W_b_Z), 0, "e4m3")).reshape(B, NB, M, C) + f64(B_b)
    Z_b_prev = np.concatenate([np.full((B, 1, M, C), NEG), Z_b[:, :-1]], axis=1)
    C_b_prev = np.concatenate([np.zeros((B, 1, M, C)), C_b[:, :-1]], axis=1)
    logits = np.concatenate([Z_a, Z_b_prev], axis=2)
    vals = np.concatenate([C_a, C_b_prev], axis=2)
    e = np.exp(logits - logits.max(axis=2, keepdims=True))
    probs = e / e.sum(axis=2, keepdims=True)
    return (probs * vals).sum(axis=2)

@@ -1,0 +1,220 @@
+from contextlib import ExitStack
+
+import concourse.mybir as mybir
+from concourse.masks import make_identity
+
+F32 = mybir.dt.float32
+BF16 = mybir.dt.bfloat16
+U32 = mybir.dt.uint32
+U8 = mybir.dt.uint8
+FP8X4 = mybir.dt.float8_e4m3fn_x4
+ALU = mybir.AluOpType
+ACT = mybir.ActivationFunctionType
+
+P = 128
+BATCHES = 4
+FEATURES = 1024
+CHANNELS = 128
+POSITIONS = 4
+GROUPS = 4
+ROWS = 128
+PASSES = 2
+HALVES = 2
+TOKENS = POSITIONS * ROWS
+WORDS = FEATURES // 2
+TERMS = 2 * POSITIONS
+NEG = -1e30
+W_KV_A, W_KV_B, W_Z_A, W_Z_B = 0, 1, 2, 3
+AHEAD = 3
+
+FLOPS = 2 * BATCHES * GROUPS * TOKENS * FEATURES * 4 * CHANNELS
+
+
+def tile_tokencompressor_pa_t_kernel(tc, H, W_a_KV, W_b_KV, W_a_Z, W_b_Z, B_a, B_b, out):
+    nc = tc.nc
+    with ExitStack() as ctx:
+        const = ctx.enter_context(tc.tile_pool(name="const", bufs=1))
+        raw_pool = ctx.enter_context(tc.tile_pool(name="raw", bufs=6))
+        grouped_pool = ctx.enter_context(tc.tile_pool(name="grouped", bufs=3))
+        code_pool = ctx.enter_context(tc.tile_pool(name="codes", bufs=8))
+        soft_pool = ctx.enter_context(tc.tile_pool(name="soft", bufs=3))
+        out_pool = ctx.enter_context(tc.tile_pool(name="outs", bufs=2))
+        psum_t = ctx.enter_context(tc.psum_pool(name="psum_t", bufs=3))
+        psum_mx = ctx.enter_context(tc.psum_pool(name="psum_mx", bufs=1))
+        psum_sum = ctx.enter_context(tc.psum_pool(name="psum_sum", bufs=1))
+
+        ident = const.tile([P, P], F32)
+        make_identity(nc, ident[:])
+
+        bias_rows = const.tile([P, CHANNELS], BF16)
+        nc.vector.memset(bias_rows[:], 0.0)
+        nc.scalar.dma_start(out=bias_rows[0:POSITIONS, :], in_=B_a)
+        nc.scalar.dma_start(out=bias_rows[POSITIONS:TERMS, :], in_=B_b)
+        bias_rows32 = const.tile([P, CHANNELS], F32)
+        nc.vector.tensor_copy(out=bias_rows32[:], in_=bias_rows[:])
+        bias_t = psum_sum.tile([P, 2, P], F32, tag="sums")
+        nc.tensor.transpose(bias_t[:, 0, :], bias_rows32[:], ident[:])
+        bias = const.tile([P, TERMS], F32)
+        nc.vector.tensor_copy(out=bias[:], in_=bias_t[:, 0, 0:TERMS])
+
+        w_raw = const.tile([P, 4, PASSES * HALVES, 2 * CHANNELS], BF16)
+        for w, weight in enumerate((W_a_KV, W_b_KV, W_a_Z, W_b_Z)):
+            nc.scalar.dma_start(
+                out=w_raw[:, w, :, :], in_=weight.rearrange("(a p e) c -> p a (e c)", a=PASSES * HALVES, e=2)
+            )
+        w_grouped = const.tile([P, 4 * PASSES, CHANNELS, 4], BF16, align_bytes=64)
+        nc.vector.tensor_copy(
+            out=w_grouped[:],
+            in_=w_raw[:].rearrange("p w (g u) (e c) -> p (w g) c (u e)", u=HALVES, e=2),
+        )
+        w_codes = const.tile([P, 4 * PASSES, CHANNELS], U32, align_bytes=64)
+        w_scales = const.tile([P, 4 * PASSES, CHANNELS], U8, align_bytes=64)
+        nc.vector.quantize_mx(
+            out=w_codes[:].rearrange("p a c -> p (a c)").bitcast(FP8X4),
+            scales=w_scales[:].rearrange("p a c -> p (a c)"),
+            in_=w_grouped[:].rearrange("p a c t -> p (a c t)"),
+        )
+
+        quantised = {}
+
+        def load_transpose_quantise(n, q):
+            raw = raw_pool.tile([P, POSITIONS, FEATURES], BF16)
+            nc.sync.dma_start(
+                out=raw[:].rearrange("r j k -> r (j k)"),
+                in_=H[n].rearrange("(r q j) k -> q r (j k)", q=GROUPS, j=POSITIONS)[q],
+            )
+            raw_words = raw[:].bitcast(F32)
+            grouped = grouped_pool.tile([P, PASSES, 4 * TOKENS], BF16, align_bytes=64)
+            for g in range(PASSES):
+                for pair in range(POSITIONS // 2):
+                    turned = psum_t.tile([P, HALVES, 2, ROWS], F32)
+                    for u in range(HALVES):
+                        for jj in range(2):
+                            first = (HALVES * g + u) * P
+                            nc.tensor.transpose(
+                                turned[:, u, jj, :], raw_words[:, 2 * pair + jj, first : first + P], ident[:]
+                            )
+                    columns = grouped[:, g, 8 * ROWS * pair : 8 * ROWS * (pair + 1)].bitcast(F32)
+                    nc.scalar.copy(
+                        out=columns.rearrange("p (c u) -> p c u", u=HALVES),
+                        in_=turned[:].rearrange("p u j r -> p (j r) u"),
+                    )
+            codes = code_pool.tile([P, PASSES, TOKENS], U32, align_bytes=64)
+            scales = code_pool.tile([P, PASSES, TOKENS], U8, align_bytes=64)
+            nc.vector.quantize_mx(
+                out=codes[:].rearrange("p g c -> p (g c)").bitcast(FP8X4),
+                scales=scales[:].rearrange("p g c -> p (g c)"),
+                in_=grouped[:].rearrange("p g c -> p (g c)"),
+            )
+            quantised[(n, q)] = (codes, scales)
+
+        def project(w, operand, tag):
+            codes, scales = operand
+            bank = psum_mx.tile([P, POSITIONS, ROWS], F32, tag=tag)
+            for g in range(PASSES):
+                nc.tensor.matmul_mx(
+                    out=bank[:].rearrange("p j r -> p (j r)"),
+                    lhsT=w_codes[:, PASSES * w + g, :].bitcast(FP8X4),
+                    lhsT_scale=w_scales[:, PASSES * w + g, :],
+                    rhs=codes[:, g, :].bitcast(FP8X4),
+                    rhs_scale=scales[:, g, :],
+                    start=(g == 0),
+                    stop=(g == PASSES - 1),
+                )
+            return bank
+
+        def windows(n, q, result):
+            own = quantised[(n, q)]
+            previous = quantised[(n, (q - 1) % GROUPS)]
+            shift = 1 if q == 0 else 0
+            kept = ROWS - shift
+
+            z_a = project(W_Z_A, own, "z_a")
+            z_b = project(W_Z_B, previous, "z_b")
+
+            top_a = soft_pool.tile([P, ROWS], F32)
+            top_b = soft_pool.tile([P, ROWS], F32)
+            nc.vector.tensor_scalar_add(out=top_a[:], in0=z_a[:, 0, :], scalar1=bias[:, 0:1])
+            nc.vector.tensor_scalar_add(
+                out=top_b[:, shift:], in0=z_b[:, 0, 0:kept], scalar1=bias[:, POSITIONS : POSITIONS + 1]
+            )
+            for j in range(1, POSITIONS):
+                nc.vector.scalar_tensor_tensor(
+                    out=top_a[:], in0=z_a[:, j, :], scalar=bias[:, j : j + 1], in1=top_a[:], op0=ALU.add, op1=ALU.max
+                )
+                nc.vector.scalar_tensor_tensor(
+                    out=top_b[:, shift:],
+                    in0=z_b[:, j, 0:kept],
+                    scalar=bias[:, POSITIONS + j : POSITIONS + j + 1],
+                    in1=top_b[:, shift:],
+                    op0=ALU.add,
+                    op1=ALU.max,
+                )
+            nc.vector.tensor_tensor(out=top_a[:, shift:], in0=top_a[:, shift:], in1=top_b[:, shift:], op=ALU.max)
+
+            weights = soft_pool.tile([P, TERMS, ROWS], F32)
+            if shift:
+                nc.vector.memset(weights[:, POSITIONS:TERMS, 0:shift], NEG)
+            for j in range(POSITIONS):
+                nc.vector.scalar_tensor_tensor(
+                    out=weights[:, j, :],
+                    in0=z_a[:, j, :],
+                    scalar=bias[:, j : j + 1],
+                    in1=top_a[:],
+                    op0=ALU.add,
+                    op1=ALU.subtract,
+                )
+                nc.vector.scalar_tensor_tensor(
+                    out=weights[:, POSITIONS + j, shift:],
+                    in0=z_b[:, j, 0:kept],
+                    scalar=bias[:, POSITIONS + j : POSITIONS + j + 1],
+                    in1=top_a[:, shift:],
+                    op0=ALU.add,
+                    op1=ALU.subtract,
+                )
+            nc.scalar.activation(out=weights[:], in_=weights[:], func=ACT.Exp)
+
+            c_a = project(W_KV_A, own, "c_a")
+            c_b = project(W_KV_B, previous, "c_b")
+            weighted = soft_pool.tile([P, TERMS, ROWS], F32)
+            if shift:
+                nc.vector.memset(weighted[:, POSITIONS:TERMS, 0:shift], 0.0)
+            nc.vector.tensor_tensor(
+                out=weighted[:, 0:POSITIONS, :], in0=c_a[:], in1=weights[:, 0:POSITIONS, :], op=ALU.mult
+            )
+            nc.vector.tensor_tensor(
+                out=weighted[:, POSITIONS:TERMS, shift:],
+                in0=c_b[:, :, 0:kept],
+                in1=weights[:, POSITIONS:TERMS, shift:],
+                op=ALU.mult,
+            )
+
+            sums = psum_sum.tile([P, 2, CHANNELS], F32, tag="sums")
+            for place, terms in enumerate((weights, weighted)):
+                for t in range(TERMS):
+                    nc.tensor.matmul(
+                        out=sums[:, place, :],
+                        lhsT=terms[:, t, :],
+                        rhs=ident[:],
+                        is_transpose=True,
+                        start=(t == 0),
+                        stop=(t == TERMS - 1),
+                    )
+            inverse = soft_pool.tile([P, CHANNELS], F32)
+            nc.vector.reciprocal(out=inverse[:], in_=sums[:, 0, :])
+            nc.vector.tensor_tensor(out=result[:, q, :], in0=sums[:, 1, :], in1=inverse[:], op=ALU.mult)
+
+        arrival = [(n, q) for n in range(BATCHES) for q in (3, 0, 1, 2)]
+        for n, q in arrival[:AHEAD]:
+            load_transpose_quantise(n, q)
+        step = 0
+        for n in range(BATCHES):
+            result = out_pool.tile([P, GROUPS, CHANNELS], F32)
+            for q in range(GROUPS):
+                if step + AHEAD < len(arrival):
+                    load_transpose_quantise(*arrival[step + AHEAD])
+                windows(n, q, result)
+                step += 1
+            nc.sync.dma_start(
+                out=out[n].rearrange("(r q) c -> r (q c)", q=GROUPS), in_=result[:].rearrange("r q c -> r (q c)")
+            )

@@ -25,7 +25,9 @@ WORDS = FEATURES // 2
 TERMS = 2 * POSITIONS
 NEG = -1e30
 W_KV_A, W_KV_B, W_Z_A, W_Z_B = 0, 1, 2, 3
-AHEAD = 3
+STEPS = BATCHES * GROUPS
+TURN_AHEAD = 3
+FETCH_AHEAD = 6
 
 FLOPS = 2 * BATCHES * GROUPS * TOKENS * FEATURES * 4 * CHANNELS
 
@@ -33,8 +35,9 @@ FLOPS = 2 * BATCHES * GROUPS * TOKENS * FEATURES * 4 * CHANNELS
 def tile_tokencompressor_pa_t_kernel(tc, H, W_a_KV, W_b_KV, W_a_Z, W_b_Z, B_a, B_b, out):
     nc = tc.nc
     with ExitStack() as ctx:
+        ctx.enter_context(tc.manual_schedule())
         const = ctx.enter_context(tc.tile_pool(name="const", bufs=1))
-        raw_pool = ctx.enter_context(tc.tile_pool(name="raw", bufs=6))
+        raw_pool = ctx.enter_context(tc.tile_pool(name="raw", bufs=FETCH_AHEAD))
         grouped_pool = ctx.enter_context(tc.tile_pool(name="grouped", bufs=3))
         code_pool = ctx.enter_context(tc.tile_pool(name="codes", bufs=8))
         soft_pool = ctx.enter_context(tc.tile_pool(name="soft", bufs=3))
@@ -42,6 +45,27 @@ def tile_tokencompressor_pa_t_kernel(tc, H, W_a_KV, W_b_KV, W_a_Z, W_b_Z, B_a, B
         psum_t = ctx.enter_context(tc.psum_pool(name="psum_t", bufs=3))
         psum_mx = ctx.enter_context(tc.psum_pool(name="psum_mx", bufs=1))
         psum_sum = ctx.enter_context(tc.psum_pool(name="psum_sum", bufs=1))
+
+        arrival = [(n, q) for n in range(BATCHES) for q in (3, 0, 1, 2)]
+        steps = [(n, q) for n in range(BATCHES) for q in range(GROUPS)]
+        raw_of = {}
+        grouped_of = {}
+        quantised = {}
+        banks = {}
+        weights_of = {}
+        weighted_of = {}
+
+        def fetch(i):
+            n, q = arrival[i]
+            raw = raw_pool.tile([P, POSITIONS, FEATURES], BF16)
+            nc.sync.dma_start(
+                out=raw[:].rearrange("r j k -> r (j k)"),
+                in_=H[n].rearrange("(r q j) k -> q r (j k)", q=GROUPS, j=POSITIONS)[q],
+            )
+            raw_of[i] = raw
+
+        for i in range(FETCH_AHEAD):
+            fetch(i)
 
         ident = const.tile([P, P], F32)
         make_identity(nc, ident[:])
@@ -75,15 +99,10 @@ def tile_tokencompressor_pa_t_kernel(tc, H, W_a_KV, W_b_KV, W_a_Z, W_b_Z, B_a, B
             in_=w_grouped[:].rearrange("p a c t -> p (a c t)"),
         )
 
-        quantised = {}
+        totals = const.tile([P, STEPS, 2, CHANNELS], F32)
 
-        def load_transpose_quantise(n, q):
-            raw = raw_pool.tile([P, POSITIONS, FEATURES], BF16)
-            nc.sync.dma_start(
-                out=raw[:].rearrange("r j k -> r (j k)"),
-                in_=H[n].rearrange("(r q j) k -> q r (j k)", q=GROUPS, j=POSITIONS)[q],
-            )
-            raw_words = raw[:].bitcast(F32)
+        def turn(i):
+            raw_words = raw_of[i][:].bitcast(F32)
             grouped = grouped_pool.tile([P, PASSES, 4 * TOKENS], BF16, align_bytes=64)
             for g in range(PASSES):
                 for pair in range(POSITIONS // 2):
@@ -99,18 +118,21 @@ def tile_tokencompressor_pa_t_kernel(tc, H, W_a_KV, W_b_KV, W_a_Z, W_b_Z, B_a, B
                         out=columns.rearrange("p (c u) -> p c u", u=HALVES),
                         in_=turned[:].rearrange("p u j r -> p (j r) u"),
                     )
+            grouped_of[i] = grouped
+
+        def quantise(i):
             codes = code_pool.tile([P, PASSES, TOKENS], U32, align_bytes=64)
             scales = code_pool.tile([P, PASSES, TOKENS], U8, align_bytes=64)
             nc.vector.quantize_mx(
                 out=codes[:].rearrange("p g c -> p (g c)").bitcast(FP8X4),
                 scales=scales[:].rearrange("p g c -> p (g c)"),
-                in_=grouped[:].rearrange("p g c -> p (g c)"),
+                in_=grouped_of[i][:].rearrange("p g c -> p (g c)"),
             )
-            quantised[(n, q)] = (codes, scales)
+            quantised[arrival[i]] = (codes, scales)
 
-        def project(w, operand, tag):
+        def project(name, w, operand, s):
             codes, scales = operand
-            bank = psum_mx.tile([P, POSITIONS, ROWS], F32, tag=tag)
+            bank = psum_mx.tile([P, POSITIONS, ROWS], F32, tag=name)
             for g in range(PASSES):
                 nc.tensor.matmul_mx(
                     out=bank[:].rearrange("p j r -> p (j r)"),
@@ -121,17 +143,30 @@ def tile_tokencompressor_pa_t_kernel(tc, H, W_a_KV, W_b_KV, W_a_Z, W_b_Z, B_a, B
                     start=(g == 0),
                     stop=(g == PASSES - 1),
                 )
-            return bank
+            banks[(name, s)] = bank
 
-        def windows(n, q, result):
-            own = quantised[(n, q)]
-            previous = quantised[(n, (q - 1) % GROUPS)]
-            shift = 1 if q == 0 else 0
+        def own_and_previous(s):
+            n, q = steps[s]
+            return quantised[(n, q)], quantised[(n, (q - 1) % GROUPS)]
+
+        def logits(s):
+            own, previous = own_and_previous(s)
+            project("z_a", W_Z_A, own, s)
+            project("z_b", W_Z_B, previous, s)
+
+        def values(s):
+            own, previous = own_and_previous(s)
+            project("c_a", W_KV_A, own, s)
+            project("c_b", W_KV_B, previous, s)
+
+        def shift_of(s):
+            return 1 if steps[s][1] == 0 else 0
+
+        def soften(s):
+            shift = shift_of(s)
             kept = ROWS - shift
-
-            z_a = project(W_Z_A, own, "z_a")
-            z_b = project(W_Z_B, previous, "z_b")
-
+            z_a = banks[("z_a", s)]
+            z_b = banks[("z_b", s)]
             top_a = soft_pool.tile([P, ROWS], F32)
             top_b = soft_pool.tile([P, ROWS], F32)
             nc.vector.tensor_scalar_add(out=top_a[:], in0=z_a[:, 0, :], scalar1=bias[:, 0:1])
@@ -153,8 +188,6 @@ def tile_tokencompressor_pa_t_kernel(tc, H, W_a_KV, W_b_KV, W_a_Z, W_b_Z, B_a, B
             nc.vector.tensor_tensor(out=top_a[:, shift:], in0=top_a[:, shift:], in1=top_b[:, shift:], op=ALU.max)
 
             weights = soft_pool.tile([P, TERMS, ROWS], F32)
-            if shift:
-                nc.vector.memset(weights[:, POSITIONS:TERMS, 0:shift], NEG)
             for j in range(POSITIONS):
                 nc.vector.scalar_tensor_tensor(
                     out=weights[:, j, :],
@@ -164,6 +197,10 @@ def tile_tokencompressor_pa_t_kernel(tc, H, W_a_KV, W_b_KV, W_a_Z, W_b_Z, B_a, B
                     op0=ALU.add,
                     op1=ALU.subtract,
                 )
+            nc.scalar.activation(out=weights[:, 0:POSITIONS, :], in_=weights[:, 0:POSITIONS, :], func=ACT.Exp)
+            if shift:
+                nc.vector.memset(weights[:, POSITIONS:TERMS, 0:shift], NEG)
+            for j in range(POSITIONS):
                 nc.vector.scalar_tensor_tensor(
                     out=weights[:, POSITIONS + j, shift:],
                     in0=z_b[:, j, 0:kept],
@@ -172,25 +209,30 @@ def tile_tokencompressor_pa_t_kernel(tc, H, W_a_KV, W_b_KV, W_a_Z, W_b_Z, B_a, B
                     op0=ALU.add,
                     op1=ALU.subtract,
                 )
-            nc.scalar.activation(out=weights[:], in_=weights[:], func=ACT.Exp)
+            nc.scalar.activation(out=weights[:, POSITIONS:TERMS, :], in_=weights[:, POSITIONS:TERMS, :], func=ACT.Exp)
+            weights_of[s] = weights
 
-            c_a = project(W_KV_A, own, "c_a")
-            c_b = project(W_KV_B, previous, "c_b")
+        def weigh(s):
+            shift = shift_of(s)
+            kept = ROWS - shift
+            weights = weights_of[s]
             weighted = soft_pool.tile([P, TERMS, ROWS], F32)
+            nc.vector.tensor_tensor(
+                out=weighted[:, 0:POSITIONS, :], in0=banks[("c_a", s)][:], in1=weights[:, 0:POSITIONS, :], op=ALU.mult
+            )
             if shift:
                 nc.vector.memset(weighted[:, POSITIONS:TERMS, 0:shift], 0.0)
             nc.vector.tensor_tensor(
-                out=weighted[:, 0:POSITIONS, :], in0=c_a[:], in1=weights[:, 0:POSITIONS, :], op=ALU.mult
-            )
-            nc.vector.tensor_tensor(
                 out=weighted[:, POSITIONS:TERMS, shift:],
-                in0=c_b[:, :, 0:kept],
+                in0=banks[("c_b", s)][:, :, 0:kept],
                 in1=weights[:, POSITIONS:TERMS, shift:],
                 op=ALU.mult,
             )
+            weighted_of[s] = weighted
 
+        def total(s):
             sums = psum_sum.tile([P, 2, CHANNELS], F32, tag="sums")
-            for place, terms in enumerate((weights, weighted)):
+            for place, terms in enumerate((weights_of[s], weighted_of[s])):
                 for t in range(TERMS):
                     nc.tensor.matmul(
                         out=sums[:, place, :],
@@ -200,21 +242,39 @@ def tile_tokencompressor_pa_t_kernel(tc, H, W_a_KV, W_b_KV, W_a_Z, W_b_Z, B_a, B
                         start=(t == 0),
                         stop=(t == TERMS - 1),
                     )
-            inverse = soft_pool.tile([P, CHANNELS], F32)
-            nc.vector.reciprocal(out=inverse[:], in_=sums[:, 0, :])
-            nc.vector.tensor_tensor(out=result[:, q, :], in0=sums[:, 1, :], in1=inverse[:], op=ALU.mult)
+            nc.scalar.copy(out=totals[:, s, :, :], in_=sums[:])
 
-        arrival = [(n, q) for n in range(BATCHES) for q in (3, 0, 1, 2)]
-        for n, q in arrival[:AHEAD]:
-            load_transpose_quantise(n, q)
-        step = 0
-        for n in range(BATCHES):
+        def divide_and_store(n):
+            mine = slice(GROUPS * n, GROUPS * (n + 1))
+            inverse = out_pool.tile([P, GROUPS, CHANNELS], F32)
+            nc.scalar.activation(out=inverse[:], in_=totals[:, mine, 0, :], func=ACT.Abs_reciprocal_sqrt)
+            nc.scalar.activation(out=inverse[:], in_=inverse[:], func=ACT.Square)
             result = out_pool.tile([P, GROUPS, CHANNELS], F32)
-            for q in range(GROUPS):
-                if step + AHEAD < len(arrival):
-                    load_transpose_quantise(*arrival[step + AHEAD])
-                windows(n, q, result)
-                step += 1
+            nc.vector.tensor_tensor(out=result[:], in0=totals[:, mine, 1, :], in1=inverse[:], op=ALU.mult)
             nc.sync.dma_start(
                 out=out[n].rearrange("(r q) c -> r (q c)", q=GROUPS), in_=result[:].rearrange("r q c -> r (q c)")
             )
+
+        for i in range(TURN_AHEAD):
+            turn(i)
+        for i in range(TURN_AHEAD - 1):
+            quantise(i)
+        logits(0)
+        for s in range(STEPS):
+            if s > 0:
+                total(s - 1)
+            values(s)
+            if s + TURN_AHEAD - 1 < STEPS:
+                quantise(s + TURN_AHEAD - 1)
+            soften(s)
+            if s + 1 < STEPS:
+                logits(s + 1)
+            weigh(s)
+            if s + FETCH_AHEAD < STEPS:
+                fetch(s + FETCH_AHEAD)
+            if s + TURN_AHEAD < STEPS:
+                turn(s + TURN_AHEAD)
+        for n in range(BATCHES - 1):
+            divide_and_store(n)
+        total(STEPS - 1)
+        divide_and_store(BATCHES - 1)

@@ -26,8 +26,10 @@ TERMS = 2 * POSITIONS
 NEG = -1e30
 W_KV_A, W_KV_B, W_Z_A, W_Z_B = 0, 1, 2, 3
 STEPS = BATCHES * GROUPS
-TURN_AHEAD = 3
+QUANTISE_AHEAD = 3
+TURN_AHEAD = 4
 FETCH_AHEAD = 6
+BANKS = PASSES * POSITIONS // 2
 
 FLOPS = 2 * BATCHES * GROUPS * TOKENS * FEATURES * 4 * CHANNELS
 
@@ -53,7 +55,7 @@ def tile_tokencompressor_pa_t_kernel(tc, H, W_a_KV, W_b_KV, W_a_Z, W_b_Z, B_a, B
         quantised = {}
         banks = {}
         weights_of = {}
-        weighted_of = {}
+        halved_of = {}
 
         def fetch(i):
             n, q = arrival[i]
@@ -101,24 +103,25 @@ def tile_tokencompressor_pa_t_kernel(tc, H, W_a_KV, W_b_KV, W_a_Z, W_b_Z, B_a, B
 
         totals = const.tile([P, STEPS, 2, CHANNELS], F32)
 
-        def turn(i):
+        def turn(i, some_banks):
             raw_words = raw_of[i][:].bitcast(F32)
-            grouped = grouped_pool.tile([P, PASSES, 4 * TOKENS], BF16, align_bytes=64)
-            for g in range(PASSES):
-                for pair in range(POSITIONS // 2):
-                    turned = psum_t.tile([P, HALVES, 2, ROWS], F32)
-                    for u in range(HALVES):
-                        for jj in range(2):
-                            first = (HALVES * g + u) * P
-                            nc.tensor.transpose(
-                                turned[:, u, jj, :], raw_words[:, 2 * pair + jj, first : first + P], ident[:]
-                            )
-                    columns = grouped[:, g, 8 * ROWS * pair : 8 * ROWS * (pair + 1)].bitcast(F32)
-                    nc.scalar.copy(
-                        out=columns.rearrange("p (c u) -> p c u", u=HALVES),
-                        in_=turned[:].rearrange("p u j r -> p (j r) u"),
-                    )
-            grouped_of[i] = grouped
+            if i not in grouped_of:
+                grouped = grouped_pool.tile([P, PASSES, 4 * TOKENS], BF16, align_bytes=64)
+                grouped_of[i] = grouped
+            for bank in some_banks:
+                g, pair = divmod(bank, POSITIONS // 2)
+                turned = psum_t.tile([P, HALVES, 2, ROWS], F32)
+                for u in range(HALVES):
+                    for jj in range(2):
+                        first = (HALVES * g + u) * P
+                        nc.tensor.transpose(
+                            turned[:, u, jj, :], raw_words[:, 2 * pair + jj, first : first + P], ident[:]
+                        )
+                columns = grouped_of[i][:, g, 8 * ROWS * pair : 8 * ROWS * (pair + 1)].bitcast(F32)
+                nc.scalar.copy(
+                    out=columns.rearrange("p (c u) -> p c u", u=HALVES),
+                    in_=turned[:].rearrange("p u j r -> p (j r) u"),
+                )
 
         def quantise(i):
             codes = code_pool.tile([P, PASSES, TOKENS], U32, align_bytes=64)
@@ -161,6 +164,13 @@ def tile_tokencompressor_pa_t_kernel(tc, H, W_a_KV, W_b_KV, W_a_Z, W_b_Z, B_a, B
 
         def shift_of(s):
             return 1 if steps[s][1] == 0 else 0
+
+        def halve(name, s, terms):
+            halved = soft_pool.tile([P, POSITIONS, ROWS], F32, tag=name + "_halved")
+            nc.gpsimd.tensor_tensor(
+                out=halved[:], in0=terms[:, 0:POSITIONS, :], in1=terms[:, POSITIONS:TERMS, :], op=ALU.add
+            )
+            halved_of[(name, s)] = halved
 
         def soften(s):
             shift = shift_of(s)
@@ -211,6 +221,7 @@ def tile_tokencompressor_pa_t_kernel(tc, H, W_a_KV, W_b_KV, W_a_Z, W_b_Z, B_a, B
                 )
             nc.scalar.activation(out=weights[:, POSITIONS:TERMS, :], in_=weights[:, POSITIONS:TERMS, :], func=ACT.Exp)
             weights_of[s] = weights
+            halve("weights", s, weights)
 
         def weigh(s):
             shift = shift_of(s)
@@ -228,19 +239,19 @@ def tile_tokencompressor_pa_t_kernel(tc, H, W_a_KV, W_b_KV, W_a_Z, W_b_Z, B_a, B
                 in1=weights[:, POSITIONS:TERMS, shift:],
                 op=ALU.mult,
             )
-            weighted_of[s] = weighted
+            halve("weighted", s, weighted)
 
         def total(s):
             sums = psum_sum.tile([P, 2, CHANNELS], F32, tag="sums")
-            for place, terms in enumerate((weights_of[s], weighted_of[s])):
-                for t in range(TERMS):
+            for place, name in enumerate(("weights", "weighted")):
+                for j in range(POSITIONS):
                     nc.tensor.matmul(
                         out=sums[:, place, :],
-                        lhsT=terms[:, t, :],
+                        lhsT=halved_of[(name, s)][:, j, :],
                         rhs=ident[:],
                         is_transpose=True,
-                        start=(t == 0),
-                        stop=(t == TERMS - 1),
+                        start=(j == 0),
+                        stop=(j == POSITIONS - 1),
                     )
             nc.scalar.copy(out=totals[:, s, :, :], in_=sums[:])
 
@@ -255,25 +266,32 @@ def tile_tokencompressor_pa_t_kernel(tc, H, W_a_KV, W_b_KV, W_a_Z, W_b_Z, B_a, B
                 out=out[n].rearrange("(r q) c -> r (q c)", q=GROUPS), in_=result[:].rearrange("r q c -> r (q c)")
             )
 
-        for i in range(TURN_AHEAD):
-            turn(i)
-        for i in range(TURN_AHEAD - 1):
+        every_bank = range(BANKS)
+        for i in range(QUANTISE_AHEAD):
+            turn(i, every_bank)
+        for i in range(QUANTISE_AHEAD):
             quantise(i)
         logits(0)
+        values(0)
+        for i in range(QUANTISE_AHEAD, TURN_AHEAD):
+            turn(i, every_bank)
         for s in range(STEPS):
-            if s > 0:
-                total(s - 1)
-            values(s)
-            if s + TURN_AHEAD - 1 < STEPS:
-                quantise(s + TURN_AHEAD - 1)
             soften(s)
+            if s + QUANTISE_AHEAD < STEPS:
+                quantise(s + QUANTISE_AHEAD)
             if s + 1 < STEPS:
                 logits(s + 1)
             weigh(s)
             if s + FETCH_AHEAD < STEPS:
                 fetch(s + FETCH_AHEAD)
             if s + TURN_AHEAD < STEPS:
-                turn(s + TURN_AHEAD)
+                turn(s + TURN_AHEAD, every_bank[: BANKS - 1])
+            if s > 0:
+                total(s - 1)
+            if s + TURN_AHEAD < STEPS:
+                turn(s + TURN_AHEAD, every_bank[BANKS - 1 :])
+            if s + 1 < STEPS:
+                values(s + 1)
         for n in range(BATCHES - 1):
             divide_and_store(n)
         total(STEPS - 1)

@@ -266,33 +266,35 @@ def tile_tokencompressor_pa_t_kernel(tc, H, W_a_KV, W_b_KV, W_a_Z, W_b_Z, B_a, B
                 out=out[n].rearrange("(r q) c -> r (q c)", q=GROUPS), in_=result[:].rearrange("r q c -> r (q c)")
             )
 
-        every_bank = range(BANKS)
+        first_banks = range(BANKS // 2)
+        last_banks = range(BANKS // 2, BANKS)
         for i in range(QUANTISE_AHEAD):
-            turn(i, every_bank)
+            turn(i, range(BANKS))
         for i in range(QUANTISE_AHEAD):
             quantise(i)
         logits(0)
-        values(0)
         for i in range(QUANTISE_AHEAD, TURN_AHEAD):
-            turn(i, every_bank)
-        for s in range(STEPS):
-            soften(s)
+            turn(i, range(BANKS))
+        for s in range(STEPS + 2):
+            if s < STEPS:
+                soften(s)
             if s + QUANTISE_AHEAD < STEPS:
                 quantise(s + QUANTISE_AHEAD)
-            if s + 1 < STEPS:
-                logits(s + 1)
-            weigh(s)
             if s + FETCH_AHEAD < STEPS:
                 fetch(s + FETCH_AHEAD)
             if s + TURN_AHEAD < STEPS:
-                turn(s + TURN_AHEAD, every_bank[: BANKS - 1])
-            if s > 0:
-                total(s - 1)
-            if s + TURN_AHEAD < STEPS:
-                turn(s + TURN_AHEAD, every_bank[BANKS - 1 :])
+                turn(s + TURN_AHEAD, first_banks)
             if s + 1 < STEPS:
-                values(s + 1)
-        for n in range(BATCHES - 1):
-            divide_and_store(n)
-        total(STEPS - 1)
+                logits(s + 1)
+            if 0 <= s - 1 < STEPS:
+                weigh(s - 1)
+            if s == STEPS:
+                for n in range(BATCHES - 1):
+                    divide_and_store(n)
+            if s >= 2:
+                total(s - 2)
+            if s + TURN_AHEAD < STEPS:
+                turn(s + TURN_AHEAD, last_banks)
+            if s < STEPS:
+                values(s)
         divide_and_store(BATCHES - 1)

@@ -55,6 +55,7 @@ def tile_tokencompressor_pa_t_kernel(tc, H, W_a_KV, W_b_KV, W_a_Z, W_b_Z, B_a, B
         quantised = {}
         banks = {}
         weights_of = {}
+        values_b_of = {}
         halved_of = {}
 
         def fetch(i):
@@ -66,7 +67,13 @@ def tile_tokencompressor_pa_t_kernel(tc, H, W_a_KV, W_b_KV, W_a_Z, W_b_Z, B_a, B
             )
             raw_of[i] = raw
 
-        for i in range(FETCH_AHEAD):
+        fetch(0)
+        w_raw = const.tile([P, 4, PASSES * HALVES, 2 * CHANNELS], BF16)
+        for w, weight in enumerate((W_a_KV, W_b_KV, W_a_Z, W_b_Z)):
+            nc.sync.dma_start(
+                out=w_raw[:, w, :, :], in_=weight.rearrange("(a p e) c -> p a (e c)", a=PASSES * HALVES, e=2)
+            )
+        for i in range(1, FETCH_AHEAD):
             fetch(i)
 
         ident = const.tile([P, P], F32)
@@ -78,16 +85,7 @@ def tile_tokencompressor_pa_t_kernel(tc, H, W_a_KV, W_b_KV, W_a_Z, W_b_Z, B_a, B
         nc.scalar.dma_start(out=bias_rows[POSITIONS:TERMS, :], in_=B_b)
         bias_rows32 = const.tile([P, CHANNELS], F32)
         nc.vector.tensor_copy(out=bias_rows32[:], in_=bias_rows[:])
-        bias_t = psum_sum.tile([P, 2, P], F32, tag="sums")
-        nc.tensor.transpose(bias_t[:, 0, :], bias_rows32[:], ident[:])
-        bias = const.tile([P, TERMS], F32)
-        nc.vector.tensor_copy(out=bias[:], in_=bias_t[:, 0, 0:TERMS])
 
-        w_raw = const.tile([P, 4, PASSES * HALVES, 2 * CHANNELS], BF16)
-        for w, weight in enumerate((W_a_KV, W_b_KV, W_a_Z, W_b_Z)):
-            nc.scalar.dma_start(
-                out=w_raw[:, w, :, :], in_=weight.rearrange("(a p e) c -> p a (e c)", a=PASSES * HALVES, e=2)
-            )
         w_grouped = const.tile([P, 4 * PASSES, CHANNELS, 4], BF16, align_bytes=64)
         nc.vector.tensor_copy(
             out=w_grouped[:],
@@ -161,6 +159,9 @@ def tile_tokencompressor_pa_t_kernel(tc, H, W_a_KV, W_b_KV, W_a_Z, W_b_Z, B_a, B
             own, previous = own_and_previous(s)
             project("c_a", W_KV_A, own, s)
             project("c_b", W_KV_B, previous, s)
+            values_b = soft_pool.tile([P, POSITIONS, ROWS], F32)
+            nc.scalar.copy(out=values_b[:], in_=banks[("c_b", s)][:])
+            values_b_of[s] = values_b
 
         def shift_of(s):
             return 1 if steps[s][1] == 0 else 0
@@ -232,10 +233,10 @@ def tile_tokencompressor_pa_t_kernel(tc, H, W_a_KV, W_b_KV, W_a_Z, W_b_Z, B_a, B
                 out=weighted[:, 0:POSITIONS, :], in0=banks[("c_a", s)][:], in1=weights[:, 0:POSITIONS, :], op=ALU.mult
             )
             if shift:
-                nc.vector.memset(weighted[:, POSITIONS:TERMS, 0:shift], 0.0)
-            nc.vector.tensor_tensor(
+                nc.gpsimd.memset(weighted[:, POSITIONS:TERMS, 0:shift], 0.0)
+            nc.gpsimd.tensor_tensor(
                 out=weighted[:, POSITIONS:TERMS, shift:],
-                in0=banks[("c_b", s)][:, :, 0:kept],
+                in0=values_b_of[s][:, :, 0:kept],
                 in1=weights[:, POSITIONS:TERMS, shift:],
                 op=ALU.mult,
             )
@@ -266,35 +267,38 @@ def tile_tokencompressor_pa_t_kernel(tc, H, W_a_KV, W_b_KV, W_a_Z, W_b_Z, B_a, B
                 out=out[n].rearrange("(r q) c -> r (q c)", q=GROUPS), in_=result[:].rearrange("r q c -> r (q c)")
             )
 
-        first_banks = range(BANKS // 2)
-        last_banks = range(BANKS // 2, BANKS)
-        for i in range(QUANTISE_AHEAD):
-            turn(i, range(BANKS))
+        every_bank = range(BANKS)
+        turn(0, every_bank)
+        bias_t = psum_sum.tile([P, 2, P], F32, tag="sums")
+        nc.tensor.transpose(bias_t[:, 0, :], bias_rows32[:], ident[:])
+        bias = const.tile([P, TERMS], F32)
+        nc.vector.tensor_copy(out=bias[:], in_=bias_t[:, 0, 0:TERMS])
+        for i in range(1, QUANTISE_AHEAD):
+            turn(i, every_bank)
         for i in range(QUANTISE_AHEAD):
             quantise(i)
         logits(0)
+        values(0)
         for i in range(QUANTISE_AHEAD, TURN_AHEAD):
-            turn(i, range(BANKS))
-        for s in range(STEPS + 2):
-            if s < STEPS:
-                soften(s)
+            turn(i, every_bank)
+        for s in range(STEPS):
+            soften(s)
             if s + QUANTISE_AHEAD < STEPS:
                 quantise(s + QUANTISE_AHEAD)
+            if s + 1 < STEPS:
+                logits(s + 1)
+            weigh(s)
             if s + FETCH_AHEAD < STEPS:
                 fetch(s + FETCH_AHEAD)
             if s + TURN_AHEAD < STEPS:
-                turn(s + TURN_AHEAD, first_banks)
-            if s + 1 < STEPS:
-                logits(s + 1)
-            if 0 <= s - 1 < STEPS:
-                weigh(s - 1)
-            if s == STEPS:
-                for n in range(BATCHES - 1):
-                    divide_and_store(n)
-            if s >= 2:
-                total(s - 2)
+                turn(s + TURN_AHEAD, every_bank[: BANKS - 1])
+            if s > 0:
+                total(s - 1)
             if s + TURN_AHEAD < STEPS:
-                turn(s + TURN_AHEAD, last_banks)
-            if s < STEPS:
-                values(s)
+                turn(s + TURN_AHEAD, every_bank[BANKS - 1 :])
+            if s + 1 < STEPS:
+                values(s + 1)
+        for n in range(BATCHES - 1):
+            divide_and_store(n)
+        total(STEPS - 1)
         divide_and_store(BATCHES - 1)

from contextlib import ExitStack

import concourse.mybir as mybir
from concourse.masks import make_identity

F32 = mybir.dt.float32
BF16 = mybir.dt.bfloat16
U32 = mybir.dt.uint32
U8 = mybir.dt.uint8
FP8X4 = mybir.dt.float8_e4m3fn_x4
ALU = mybir.AluOpType
ACT = mybir.ActivationFunctionType

P = 128
BATCHES = 4
FEATURES = 1024
CHANNELS = 128
POSITIONS = 4
GROUPS = 4
ROWS = 128
PASSES = 2
HALVES = 2
TOKENS = POSITIONS * ROWS
WORDS = FEATURES // 2
TERMS = 2 * POSITIONS
NEG = -1e30
W_KV_A, W_KV_B, W_Z_A, W_Z_B = 0, 1, 2, 3
STEPS = BATCHES * GROUPS
QUANTISE_AHEAD = 3
TURN_AHEAD = 4
FETCH_AHEAD = 6
BANKS = PASSES * POSITIONS // 2

FLOPS = 2 * BATCHES * GROUPS * TOKENS * FEATURES * 4 * CHANNELS


def tile_tokencompressor_pa_t_kernel(tc, H, W_a_KV, W_b_KV, W_a_Z, W_b_Z, B_a, B_b, out):
    nc = tc.nc
    with ExitStack() as ctx:
        ctx.enter_context(tc.manual_schedule())
        const = ctx.enter_context(tc.tile_pool(name="const", bufs=1))
        raw_pool = ctx.enter_context(tc.tile_pool(name="raw", bufs=FETCH_AHEAD))
        grouped_pool = ctx.enter_context(tc.tile_pool(name="grouped", bufs=3))
        code_pool = ctx.enter_context(tc.tile_pool(name="codes", bufs=8))
        soft_pool = ctx.enter_context(tc.tile_pool(name="soft", bufs=3))
        out_pool = ctx.enter_context(tc.tile_pool(name="outs", bufs=2))
        psum_t = ctx.enter_context(tc.psum_pool(name="psum_t", bufs=3))
        psum_mx = ctx.enter_context(tc.psum_pool(name="psum_mx", bufs=1))
        psum_sum = ctx.enter_context(tc.psum_pool(name="psum_sum", bufs=1))

        arrival = [(n, q) for n in range(BATCHES) for q in (3, 0, 1, 2)]
        steps = [(n, q) for n in range(BATCHES) for q in range(GROUPS)]
        raw_of = {}
        grouped_of = {}
        quantised = {}
        banks = {}
        weights_of = {}
        values_b_of = {}
        halved_of = {}

        def fetch(i):
            n, q = arrival[i]
            raw = raw_pool.tile([P, POSITIONS, FEATURES], BF16)
            nc.sync.dma_start(
                out=raw[:].rearrange("r j k -> r (j k)"),
                in_=H[n].rearrange("(r q j) k -> q r (j k)", q=GROUPS, j=POSITIONS)[q],
            )
            raw_of[i] = raw

        fetch(0)
        w_raw = const.tile([P, 4, PASSES * HALVES, 2 * CHANNELS], BF16)
        for w, weight in enumerate((W_a_KV, W_b_KV, W_a_Z, W_b_Z)):
            nc.sync.dma_start(
                out=w_raw[:, w, :, :], in_=weight.rearrange("(a p e) c -> p a (e c)", a=PASSES * HALVES, e=2)
            )
        for i in range(1, FETCH_AHEAD):
            fetch(i)

        ident = const.tile([P, P], F32)
        make_identity(nc, ident[:])

        bias_rows = const.tile([P, CHANNELS], BF16)
        nc.vector.memset(bias_rows[:], 0.0)
        nc.scalar.dma_start(out=bias_rows[0:POSITIONS, :], in_=B_a)
        nc.scalar.dma_start(out=bias_rows[POSITIONS:TERMS, :], in_=B_b)
        bias_rows32 = const.tile([P, CHANNELS], F32)
        nc.vector.tensor_copy(out=bias_rows32[:], in_=bias_rows[:])

        w_grouped = const.tile([P, 4 * PASSES, CHANNELS, 4], BF16, align_bytes=64)
        nc.vector.tensor_copy(
            out=w_grouped[:],
            in_=w_raw[:].rearrange("p w (g u) (e c) -> p (w g) c (u e)", u=HALVES, e=2),
        )
        w_codes = const.tile([P, 4 * PASSES, CHANNELS], U32, align_bytes=64)
        w_scales = const.tile([P, 4 * PASSES, CHANNELS], U8, align_bytes=64)
        nc.vector.quantize_mx(
            out=w_codes[:].rearrange("p a c -> p (a c)").bitcast(FP8X4),
            scales=w_scales[:].rearrange("p a c -> p (a c)"),
            in_=w_grouped[:].rearrange("p a c t -> p (a c t)"),
        )

        totals = const.tile([P, STEPS, 2, CHANNELS], F32)

        def turn(i, some_banks):
            raw_words = raw_of[i][:].bitcast(F32)
            if i not in grouped_of:
                grouped = grouped_pool.tile([P, PASSES, 4 * TOKENS], BF16, align_bytes=64)
                grouped_of[i] = grouped
            for bank in some_banks:
                g, pair = divmod(bank, POSITIONS // 2)
                turned = psum_t.tile([P, HALVES, 2, ROWS], F32)
                for u in range(HALVES):
                    for jj in range(2):
                        first = (HALVES * g + u) * P
                        nc.tensor.transpose(
                            turned[:, u, jj, :], raw_words[:, 2 * pair + jj, first : first + P], ident[:]
                        )
                columns = grouped_of[i][:, g, 8 * ROWS * pair : 8 * ROWS * (pair + 1)].bitcast(F32)
                nc.scalar.copy(
                    out=columns.rearrange("p (c u) -> p c u", u=HALVES),
                    in_=turned[:].rearrange("p u j r -> p (j r) u"),
                )

        def quantise(i):
            codes = code_pool.tile([P, PASSES, TOKENS], U32, align_bytes=64)
            scales = code_pool.tile([P, PASSES, TOKENS], U8, align_bytes=64)
            nc.vector.quantize_mx(
                out=codes[:].rearrange("p g c -> p (g c)").bitcast(FP8X4),
                scales=scales[:].rearrange("p g c -> p (g c)"),
                in_=grouped_of[i][:].rearrange("p g c -> p (g c)"),
            )
            quantised[arrival[i]] = (codes, scales)

        def project(name, w, operand, s):
            codes, scales = operand
            bank = psum_mx.tile([P, POSITIONS, ROWS], F32, tag=name)
            for g in range(PASSES):
                nc.tensor.matmul_mx(
                    out=bank[:].rearrange("p j r -> p (j r)"),
                    lhsT=w_codes[:, PASSES * w + g, :].bitcast(FP8X4),
                    lhsT_scale=w_scales[:, PASSES * w + g, :],
                    rhs=codes[:, g, :].bitcast(FP8X4),
                    rhs_scale=scales[:, g, :],
                    start=(g == 0),
                    stop=(g == PASSES - 1),
                )
            banks[(name, s)] = bank

        def own_and_previous(s):
            n, q = steps[s]
            return quantised[(n, q)], quantised[(n, (q - 1) % GROUPS)]

        def logits(s):
            own, previous = own_and_previous(s)
            project("z_a", W_Z_A, own, s)
            project("z_b", W_Z_B, previous, s)

        def values(s):
            own, previous = own_and_previous(s)
            project("c_a", W_KV_A, own, s)
            project("c_b", W_KV_B, previous, s)
            values_b = soft_pool.tile([P, POSITIONS, ROWS], F32)
            nc.scalar.copy(out=values_b[:], in_=banks[("c_b", s)][:])
            values_b_of[s] = values_b

        def shift_of(s):
            return 1 if steps[s][1] == 0 else 0

        def halve(name, s, terms):
            halved = soft_pool.tile([P, POSITIONS, ROWS], F32, tag=name + "_halved")
            nc.gpsimd.tensor_tensor(
                out=halved[:], in0=terms[:, 0:POSITIONS, :], in1=terms[:, POSITIONS:TERMS, :], op=ALU.add
            )
            halved_of[(name, s)] = halved

        def soften(s):
            shift = shift_of(s)
            kept = ROWS - shift
            z_a = banks[("z_a", s)]
            z_b = banks[("z_b", s)]
            top_a = soft_pool.tile([P, ROWS], F32)
            top_b = soft_pool.tile([P, ROWS], F32)
            nc.vector.tensor_scalar_add(out=top_a[:], in0=z_a[:, 0, :], scalar1=bias[:, 0:1])
            nc.vector.tensor_scalar_add(
                out=top_b[:, shift:], in0=z_b[:, 0, 0:kept], scalar1=bias[:, POSITIONS : POSITIONS + 1]
            )
            for j in range(1, POSITIONS):
                nc.vector.scalar_tensor_tensor(
                    out=top_a[:], in0=z_a[:, j, :], scalar=bias[:, j : j + 1], in1=top_a[:], op0=ALU.add, op1=ALU.max
                )
                nc.vector.scalar_tensor_tensor(
                    out=top_b[:, shift:],
                    in0=z_b[:, j, 0:kept],
                    scalar=bias[:, POSITIONS + j : POSITIONS + j + 1],
                    in1=top_b[:, shift:],
                    op0=ALU.add,
                    op1=ALU.max,
                )
            nc.vector.tensor_tensor(out=top_a[:, shift:], in0=top_a[:, shift:], in1=top_b[:, shift:], op=ALU.max)

            weights = soft_pool.tile([P, TERMS, ROWS], F32)
            for j in range(POSITIONS):
                nc.vector.scalar_tensor_tensor(
                    out=weights[:, j, :],
                    in0=z_a[:, j, :],
                    scalar=bias[:, j : j + 1],
                    in1=top_a[:],
                    op0=ALU.add,
                    op1=ALU.subtract,
                )
            nc.scalar.activation(out=weights[:, 0:POSITIONS, :], in_=weights[:, 0:POSITIONS, :], func=ACT.Exp)
            if shift:
                nc.vector.memset(weights[:, POSITIONS:TERMS, 0:shift], NEG)
            for j in range(POSITIONS):
                nc.vector.scalar_tensor_tensor(
                    out=weights[:, POSITIONS + j, shift:],
                    in0=z_b[:, j, 0:kept],
                    scalar=bias[:, POSITIONS + j : POSITIONS + j + 1],
                    in1=top_a[:, shift:],
                    op0=ALU.add,
                    op1=ALU.subtract,
                )
            nc.scalar.activation(out=weights[:, POSITIONS:TERMS, :], in_=weights[:, POSITIONS:TERMS, :], func=ACT.Exp)
            weights_of[s] = weights
            halve("weights", s, weights)

        def weigh(s):
            shift = shift_of(s)
            kept = ROWS - shift
            weights = weights_of[s]
            weighted = soft_pool.tile([P, TERMS, ROWS], F32)
            nc.vector.tensor_tensor(
                out=weighted[:, 0:POSITIONS, :], in0=banks[("c_a", s)][:], in1=weights[:, 0:POSITIONS, :], op=ALU.mult
            )
            if shift:
                nc.gpsimd.memset(weighted[:, POSITIONS:TERMS, 0:shift], 0.0)
            nc.gpsimd.tensor_tensor(
                out=weighted[:, POSITIONS:TERMS, shift:],
                in0=values_b_of[s][:, :, 0:kept],
                in1=weights[:, POSITIONS:TERMS, shift:],
                op=ALU.mult,
            )
            halve("weighted", s, weighted)

        def total(s):
            sums = psum_sum.tile([P, 2, CHANNELS], F32, tag="sums")
            for place, name in enumerate(("weights", "weighted")):
                for j in range(POSITIONS):
                    nc.tensor.matmul(
                        out=sums[:, place, :],
                        lhsT=halved_of[(name, s)][:, j, :],
                        rhs=ident[:],
                        is_transpose=True,
                        start=(j == 0),
                        stop=(j == POSITIONS - 1),
                    )
            nc.scalar.copy(out=totals[:, s, :, :], in_=sums[:])

        def divide_and_store(n):
            mine = slice(GROUPS * n, GROUPS * (n + 1))
            inverse = out_pool.tile([P, GROUPS, CHANNELS], F32)
            nc.scalar.activation(out=inverse[:], in_=totals[:, mine, 0, :], func=ACT.Abs_reciprocal_sqrt)
            nc.scalar.activation(out=inverse[:], in_=inverse[:], func=ACT.Square)
            result = out_pool.tile([P, GROUPS, CHANNELS], F32)
            nc.vector.tensor_tensor(out=result[:], in0=totals[:, mine, 1, :], in1=inverse[:], op=ALU.mult)
            nc.sync.dma_start(
                out=out[n].rearrange("(r q) c -> r (q c)", q=GROUPS), in_=result[:].rearrange("r q c -> r (q c)")
            )

        every_bank = range(BANKS)
        turn(0, every_bank)
        bias_t = psum_sum.tile([P, 2, P], F32, tag="sums")
        nc.tensor.transpose(bias_t[:, 0, :], bias_rows32[:], ident[:])
        bias = const.tile([P, TERMS], F32)
        nc.vector.tensor_copy(out=bias[:], in_=bias_t[:, 0, 0:TERMS])
        for i in range(1, QUANTISE_AHEAD):
            turn(i, every_bank)
        for i in range(QUANTISE_AHEAD):
            quantise(i)
        logits(0)
        values(0)
        for i in range(QUANTISE_AHEAD, TURN_AHEAD):
            turn(i, every_bank)
        for s in range(STEPS):
            soften(s)
            if s + QUANTISE_AHEAD < STEPS:
                quantise(s + QUANTISE_AHEAD)
            if s + 1 < STEPS:
                logits(s + 1)
            weigh(s)
            if s + FETCH_AHEAD < STEPS:
                fetch(s + FETCH_AHEAD)
            if s + TURN_AHEAD < STEPS:
                turn(s + TURN_AHEAD, every_bank[: BANKS - 1])
            if s > 0:
                total(s - 1)
            if s + TURN_AHEAD < STEPS:
                turn(s + TURN_AHEAD, every_bank[BANKS - 1 :])
            if s + 1 < STEPS:
                values(s + 1)
        for n in range(BATCHES - 1):
            divide_and_store(n)
        total(STEPS - 1)
        divide_and_store(BATCHES - 1)
